import numpy as np
import ml_dtypes


def mxq(x, axis, fmt="e4m3"):
    dtype, down = {"e4m3": (ml_dtypes.float8_e4m3fn, 7), "e5m2": (ml_dtypes.float8_e5m2, 14)}[fmt]
    v = np.moveaxis(np.asarray(x, np.float32).astype(ml_dtypes.bfloat16).astype(np.float64), axis, -1)
    blocks = v.reshape(v.shape[:-1] + (-1, 32))
    amax = np.abs(blocks).max(-1, keepdims=True)
    byte = np.maximum(np.where(amax > 0, np.frexp(amax)[1] - 1 + 127, 0) - down, 1)
    scale = np.exp2(byte - 127.0)
    codes = (blocks / scale).astype(np.float32).astype(dtype).astype(np.float64)
    return np.moveaxis((codes * scale).reshape(v.shape), -1, axis)


WIDE = False


def mx_kscale(k):
    if not WIDE:
        return np.ones(k)
    levels = np.array([10, -10, 5, -5, 0])
    a = np.random.permutation(np.resize(levels, k // 512 * 4)).reshape(k // 512, 4)
    idx = np.arange(k)
    return np.exp2(a[idx // 512, idx % 128 // 32])


BF16 = ml_dtypes.bfloat16


def bf(x):
    return np.asarray(x, np.float32).astype(BF16)


def f64(x):
    return np.asarray(x).astype(np.float64)


B, N, D, H, DK, DV = 4, 1024, 512, 8, 64, 64


def xnorm(x, g):
    n = np.sqrt(np.sum(x * x, axis=-1, keepdims=True))
    return x * g / n


def setup_inputs():
    s = mx_kscale(D)
    return {
        "queries": bf(np.random.standard_normal((B, N, D)) * s),
        "Wq": bf(np.random.standard_normal((D, H * DK)) / np.sqrt(D) / s[:, None]),
        "bq": bf(np.random.standard_normal(H * DK) * 0.1),
        "gamma": bf(np.random.standard_normal((1, H, 1, 1)) * 2.0),
    }


def reference(queries, Wq, bq, gamma):
    q = ((mxq(f64(queries), 2, "e4m3") @ mxq(f64(Wq), 0, "e4m3")) + f64(bq)).reshape(B, N, H, DK)
    return xnorm(q.transpose(0, 2, 1, 3), f64(gamma))

@@ -1,0 +1,273 @@
+from contextlib import ExitStack
+
+import concourse.mybir as mybir
+from concourse.masks import make_identity
+
+F32 = mybir.dt.float32
+BF16 = mybir.dt.bfloat16
+U32 = mybir.dt.uint32
+U8 = mybir.dt.uint8
+FP8X4 = mybir.dt.float8_e4m3fn_x4
+ACT = mybir.ActivationFunctionType
+ALU = mybir.AluOpType
+AX = mybir.AxisListType
+
+B, N, D, H, DK = 4, 1024, 512, 8, 64
+P = 128
+J = N // P
+FLOPS = 2 * B * N * D * H * DK
+
+PIN = False
+NV = 10
+MG = 10
+MV_LAST = 10
+NU = 16
+
+
+def tile_ufoattention_pb_kernel(tc, queries, Wq, bq, gamma, out):
+    nc = tc.nc
+    with ExitStack() as ctx:
+        const = ctx.enter_context(tc.tile_pool(name="const", bufs=1))
+        xq = ctx.enter_context(tc.tile_pool(name="xq", bufs=2))
+        outp = ctx.enter_context(tc.tile_pool(name="outp", bufs=5))
+        small = ctx.enter_context(tc.tile_pool(name="small", bufs=4))
+        psum = ctx.enter_context(tc.psum_pool(name="psum", bufs=2))
+        if PIN:
+            ctx.enter_context(tc.manual_schedule())
+
+        bstage = const.tile([1, 520], BF16)
+        nc.sync.dma_start(out=bstage[0:1, 0:512], in_=bq.rearrange("(o n) -> o n", o=1))
+        nc.sync.dma_start(out=bstage[0:1, 512:520], in_=gamma.rearrange("a h b c -> a (h b c)"))
+        x_sb = [const.tile([P, J * D], BF16, name="x%d" % b) for b in range(B)]
+        qv = [queries[b].rearrange("(p j) k -> p (j k)", j=J) for b in range(B)]
+        w_raw = const.tile([P, 4, 512], BF16)
+        nc.sync.dma_start(out=x_sb[0][:, 0:1024], in_=qv[0][:, 0:1024])
+        nc.sync.dma_start(out=x_sb[0][:, 1024:2048], in_=qv[0][:, 1024:2048])
+        nc.sync.dma_start(
+            out=w_raw[:].rearrange("q (u e) n -> q u (e n)", u=2),
+            in_=Wq.rearrange("(u q e) n -> q u (e n)", u=2, e=2),
+        )
+        nc.sync.dma_start(out=x_sb[0][:, 2048:4096], in_=qv[0][:, 2048:4096])
+        nc.sync.dma_start(out=x_sb[1][:, 0:2048], in_=qv[1][:, 0:2048])
+        nc.sync.dma_start(out=x_sb[1][:, 2048:4096], in_=qv[1][:, 2048:4096])
+        nc.sync.dma_start(out=x_sb[2][:], in_=qv[2])
+        nc.sync.dma_start(out=x_sb[3][:], in_=qv[3])
+
+        ident = const.tile([P, P], F32)
+        make_identity(nc, ident[:])
+        one1 = const.tile([P, 1], F32)
+        nc.vector.memset(one1[:], 1.0)
+        warm = const.tile([P, 1], F32)
+        nc.scalar.activation(out=warm[:], in_=one1[:], func=ACT.Abs_reciprocal_sqrt)
+        brow = const.tile([P, 576], BF16)
+        nc.vector.memset(brow[:], 0.0)
+        ones = const.tile([P, P], BF16)
+        nc.vector.memset(ones[:], 1.0)
+        nc.vector.tensor_copy(out=brow[0:1, 0:520], in_=bstage[0:1, :])
+        b_bc = const.tile([P, 512], F32)
+        g_bc = const.tile([P, 64], F32)
+        w_grp = const.tile([P, 512, 4], BF16, align_bytes=64)
+        w_codes = const.tile([P, 512], U32, align_bytes=64)
+        w_scales = const.tile([P, 512], U8, align_bytes=64)
+
+        def w_prep(g):
+            cols = slice(g * 128, (g + 1) * 128)
+            nc.vector.tensor_copy(
+                out=w_grp[:, cols, :], in_=w_raw[:, :, cols].rearrange("q t n -> q n t")
+            )
+            nc.vector.quantize_mx(
+                out=w_codes[:, cols].bitcast(FP8X4),
+                scales=w_scales[:, cols],
+                in_=w_grp[:, cols, :].rearrange("q n t -> q (n t)"),
+            )
+
+        xt = {}
+        tps = {}
+
+        def x_tiles(b):
+            if b not in xt:
+                xg = xq.tile([P, J * P * 4], BF16, tag="xg", align_bytes=64)
+                xc = xq.tile([P, J * P], U32, tag="xc", align_bytes=64)
+                xs = xq.tile([P, J * P], U8, tag="xs", align_bytes=64)
+                xt[b] = (xg, xc, xs)
+            return xt[b]
+
+        def tr(b, c):
+            xw = x_sb[b][:].bitcast(F32)
+            tp = psum.tile([P, 2, 2, P], F32, tag="tp", bufs=2)
+            for jj in range(2):
+                for u in range(2):
+                    o0 = (2 * c + jj) * 256 + u * 128
+                    nc.tensor.transpose(tp[:, jj, u, :], xw[:, o0 : o0 + 128], ident[:])
+            tps[(b, c)] = tp
+
+        def cp(b, c):
+            xg = x_tiles(b)[0]
+            nc.scalar.copy(
+                out=xg[:].bitcast(F32)[:, c * 512 : (c + 1) * 512].rearrange(
+                    "p (jj n u) -> p jj n u", jj=2, u=2
+                ),
+                in_=tps[(b, c)][:].rearrange("p jj u n -> p jj n u"),
+            )
+
+        def qz(b, c):
+            xg, xc, xs = x_tiles(b)
+            nc.vector.quantize_mx(
+                out=xc[:, c * 256 : (c + 1) * 256].bitcast(FP8X4),
+                scales=xs[:, c * 256 : (c + 1) * 256],
+                in_=xg[:, c * 1024 : (c + 1) * 1024],
+            )
+
+        accs = {}
+        st = {}
+
+        def mx(s):
+            b, g = divmod(s, 4)
+            xc, xs = x_tiles(b)[1:]
+            wcols = slice(g * 128, (g + 1) * 128)
+            for k in range(2):
+                acc = psum.tile([P, 4, P], F32, tag="acc", bufs=6)
+                for jj in range(4):
+                    tcols = slice((4 * k + jj) * P, (4 * k + jj + 1) * P)
+                    nc.tensor.matmul_mx(
+                        out=acc[:, jj, :],
+                        lhsT=xc[:, tcols].bitcast(FP8X4),
+                        lhsT_scale=xs[:, tcols],
+                        rhs=w_codes[:, wcols].bitcast(FP8X4),
+                        rhs_scale=w_scales[:, wcols],
+                        start=True,
+                        stop=True,
+                    )
+                accs[(s, k)] = acc
+
+        def e1(s):
+            g = s % 4
+            o = outp.tile([P, 2, J, DK], F32, tag="o")
+            bias = (
+                b_bc[:, g * 128 : (g + 1) * 128]
+                .rearrange("p (h d) -> p h d", h=2)
+                .unsqueeze(1)
+                .to_broadcast([P, 4, 2, DK])
+            )
+            for k in range(2):
+                nc.vector.tensor_tensor(
+                    out=o[:, :, 4 * k : 4 * k + 4, :].rearrange("p h j d -> p j h d"),
+                    in0=accs[(s, k)][:].rearrange("p j (h d) -> p j h d", h=2),
+                    in1=bias,
+                    op=ALU.add,
+                )
+            ss = small.tile([P, 32], F32, tag="ss")
+            stats = small.tile([P, NV // 2, 6], F32, tag="stats")
+            rs = small.tile([P, 16], F32, tag="rs")
+            rn = small.tile([P, 16], F32, tag="rn")
+            st[s] = (o, o[:].rearrange("p h j d -> p (h j) d"), ss, stats, rs, rn)
+
+        def bn(s):
+            og, stats = st[s][1], st[s][3]
+            for m in range(NV // 2):
+                nc.vector.bn_stats(
+                    out=stats[:, m, :],
+                    in_=og[:, 2 * m : 2 * m + 2, :].rearrange("p g d -> p d g"),
+                )
+
+        def sq(s):
+            og, ss = st[s][1], st[s][2]
+            for i in range(NV, 16):
+                junk = small.tile([P, DK], F32, tag="junk")
+                nc.scalar.activation(
+                    out=junk[:], in_=og[:, i, :], func=ACT.Square,
+                    accum_out=ss[:, 16 + i - NV : 17 + i - NV],
+                )
+
+        def red(s):
+            ss, stats = st[s][2], st[s][3]
+            sv = stats[:].rearrange("p n (a c) -> p n a c", c=3)
+            nc.vector.scalar_tensor_tensor(
+                out=sv[:, :, :, 1:2], in0=sv[:, :, :, 1:2], scalar=64.0, in1=sv[:, :, :, 1:2],
+                op0=ALU.mult, op1=ALU.mult,
+            )
+            nc.vector.tensor_reduce(
+                out=ss[:, 16 - NV : 16].rearrange("p (n a) -> p n a", a=2),
+                in_=sv[:, :, :, 1:3], axis=AX.X, op=ALU.add,
+            )
+
+        def ars(s):
+            g = s % 4
+            ss, rs, rn = st[s][2], st[s][4], st[s][5]
+            nc.scalar.activation(
+                out=rs[:], in_=ss[:, 16 - NV : 32 - NV], func=ACT.Abs_reciprocal_sqrt
+            )
+            for hh in range(2):
+                nc.scalar.activation(
+                    out=rn[:, hh * J : (hh + 1) * J], in_=rs[:, hh * J : (hh + 1) * J],
+                    func=ACT.Copy, scale=g_bc[:, 2 * g + hh : 2 * g + hh + 1],
+                )
+
+        def e4(s):
+            og, rn = st[s][1], st[s][5]
+            last = s == NU - 1
+            wide = MV_LAST if last else MG
+            if wide > 0:
+                eng = nc.vector if last else nc.gpsimd
+                eng.tensor_tensor(
+                    out=og[:, 0:wide, :], in0=og[:, 0:wide, :],
+                    in1=rn[:, 0:wide].unsqueeze(2).to_broadcast([P, wide, DK]), op=ALU.mult,
+                )
+            for i in range(wide, 16):
+                nc.scalar.activation(
+                    out=og[:, i, :], in_=og[:, i, :], func=ACT.Copy, scale=rn[:, i : i + 1]
+                )
+
+        def store(s):
+            b, g = divmod(s, 4)
+            nc.sync.dma_start(
+                out=out[b, 2 * g : 2 * g + 2].rearrange("h (p j) d -> p h (j d)", j=J),
+                in_=st[s][0][:].rearrange("p h j d -> p h (j d)"),
+            )
+
+        tr(0, 0)
+        cp(0, 0)
+        qz(0, 0)
+        tr(0, 1)
+        cp(0, 1)
+        qz(0, 1)
+        pb = psum.tile([P, 512], F32, tag="acc", bufs=6)
+        nc.tensor.matmul(pb[:], lhsT=ones[:], rhs=brow[:, 0:512], start=True, stop=True)
+        nc.scalar.copy(out=b_bc[:], in_=pb[:])
+        pg = psum.tile([P, 64], F32, tag="acc", bufs=6)
+        nc.tensor.matmul(pg[:], lhsT=ones[:], rhs=brow[:, 512:576], start=True, stop=True)
+        nc.scalar.copy(out=g_bc[:], in_=pg[:])
+        w_prep(0)
+        tr(0, 2)
+        cp(0, 2)
+        tr(0, 3)
+        cp(0, 3)
+        w_prep(1)
+        qz(0, 2)
+        qz(0, 3)
+        mx(0)
+
+        for s in range(NU + 1):
+            chunks = [i for i in ([0, 1] if s == 0 else [s + 1]) if i < 12]
+            chunks = [(i // 4 + 1, i % 4) for i in chunks]
+            if s + 1 < NU:
+                mx(s + 1)
+            for bc in chunks:
+                tr(bc[0], bc[1])
+            if s < NU:
+                e1(s)
+                bn(s)
+            if s > 0:
+                e4(s - 1)
+                store(s - 1)
+            for bc in chunks:
+                cp(bc[0], bc[1])
+            if s < NU:
+                sq(s)
+                red(s)
+            for bc in chunks:
+                qz(bc[0], bc[1])
+            if s < 2:
+                w_prep(s + 2)
+            if s < NU:
+                ars(s)

@@ -18,9 +18,9 @@ J = N // P
 FLOPS = 2 * B * N * D * H * DK
 
 PIN = False
-NV = 10
-MG = 10
-MV_LAST = 10
+NV = 14
+MG = 0
+MV_LAST = 8
 NU = 16
 
 

@@ -18,9 +18,9 @@ J = N // P
 FLOPS = 2 * B * N * D * H * DK
 
 PIN = False
-NV = 14
-MG = 0
-MV_LAST = 8
+NV = 8
+MG = 10
+MV_LAST = 10
 NU = 16
 
 
@@ -118,6 +118,10 @@ def tile_ufoattention_pb_kernel(tc, queries, Wq, bq, gamma, out):
                 in_=xg[:, c * 1024 : (c + 1) * 1024],
             )
 
+        def qz_all(b):
+            xg, xc, xs = x_tiles(b)
+            nc.vector.quantize_mx(out=xc[:].bitcast(FP8X4), scales=xs[:], in_=xg[:])
+
         accs = {}
         st = {}
 
@@ -182,9 +186,8 @@ def tile_ufoattention_pb_kernel(tc, queries, Wq, bq, gamma, out):
         def red(s):
             ss, stats = st[s][2], st[s][3]
             sv = stats[:].rearrange("p n (a c) -> p n a c", c=3)
-            nc.vector.scalar_tensor_tensor(
-                out=sv[:, :, :, 1:2], in0=sv[:, :, :, 1:2], scalar=64.0, in1=sv[:, :, :, 1:2],
-                op0=ALU.mult, op1=ALU.mult,
+            nc.scalar.activation(
+                out=sv[:, :, :, 1:2], in_=sv[:, :, :, 1:2], func=ACT.Square, scale=8.0
             )
             nc.vector.tensor_reduce(
                 out=ss[:, 16 - NV : 16].rearrange("p (n a) -> p n a", a=2),
@@ -266,7 +269,8 @@ def tile_ufoattention_pb_kernel(tc, queries, Wq, bq, gamma, out):
                 sq(s)
                 red(s)
             for bc in chunks:
-                qz(bc[0], bc[1])
+                if bc[1] == 3:
+                    qz_all(bc[0])
             if s < 2:
                 w_prep(s + 2)
             if s < NU:

@@ -19,7 +19,7 @@ FLOPS = 2 * B * N * D * H * DK
 
 PIN = False
 NV = 8
-MG = 10
+MG = 13
 MV_LAST = 10
 NU = 16
 

@@ -18,8 +18,8 @@ J = N // P
 FLOPS = 2 * B * N * D * H * DK
 
 PIN = False
-NV = 8
-MG = 13
+NV = 10
+MG = 10
 MV_LAST = 10
 NU = 16
 

@@ -29,8 +29,8 @@ def tile_ufoattention_pb_kernel(tc, queries, Wq, bq, gamma, out):
     with ExitStack() as ctx:
         const = ctx.enter_context(tc.tile_pool(name="const", bufs=1))
         xq = ctx.enter_context(tc.tile_pool(name="xq", bufs=2))
-        outp = ctx.enter_context(tc.tile_pool(name="outp", bufs=5))
-        small = ctx.enter_context(tc.tile_pool(name="small", bufs=4))
+        outp = ctx.enter_context(tc.tile_pool(name="outp", bufs=10))
+        small = ctx.enter_context(tc.tile_pool(name="small", bufs=8))
         psum = ctx.enter_context(tc.psum_pool(name="psum", bufs=2))
         if PIN:
             ctx.enter_context(tc.manual_schedule())

@@ -29,8 +29,8 @@ def tile_ufoattention_pb_kernel(tc, queries, Wq, bq, gamma, out):
     with ExitStack() as ctx:
         const = ctx.enter_context(tc.tile_pool(name="const", bufs=1))
         xq = ctx.enter_context(tc.tile_pool(name="xq", bufs=2))
-        outp = ctx.enter_context(tc.tile_pool(name="outp", bufs=10))
-        small = ctx.enter_context(tc.tile_pool(name="small", bufs=8))
+        outp = ctx.enter_context(tc.tile_pool(name="outp", bufs=5))
+        small = ctx.enter_context(tc.tile_pool(name="small", bufs=4))
         psum = ctx.enter_context(tc.psum_pool(name="psum", bufs=2))
         if PIN:
             ctx.enter_context(tc.manual_schedule())
@@ -94,7 +94,7 @@ def tile_ufoattention_pb_kernel(tc, queries, Wq, bq, gamma, out):
 
         def tr(b, c):
             xw = x_sb[b][:].bitcast(F32)
-            tp = psum.tile([P, 2, 2, P], F32, tag="tp", bufs=2)
+            tp = psum.tile([P, 2, 2, P], F32, tag="tp", bufs=4)
             for jj in range(2):
                 for u in range(2):
                     o0 = (2 * c + jj) * 256 + u * 128
@@ -130,7 +130,7 @@ def tile_ufoattention_pb_kernel(tc, queries, Wq, bq, gamma, out):
             xc, xs = x_tiles(b)[1:]
             wcols = slice(g * 128, (g + 1) * 128)
             for k in range(2):
-                acc = psum.tile([P, 4, P], F32, tag="acc", bufs=6)
+                acc = psum.tile([P, 4, P], F32, tag="acc", bufs=4)
                 for jj in range(4):
                     tcols = slice((4 * k + jj) * P, (4 * k + jj + 1) * P)
                     nc.tensor.matmul_mx(
@@ -234,10 +234,10 @@ def tile_ufoattention_pb_kernel(tc, queries, Wq, bq, gamma, out):
         tr(0, 1)
         cp(0, 1)
         qz(0, 1)
-        pb = psum.tile([P, 512], F32, tag="acc", bufs=6)
+        pb = psum.tile([P, 512], F32, tag="acc", bufs=4)
         nc.tensor.matmul(pb[:], lhsT=ones[:], rhs=brow[:, 0:512], start=True, stop=True)
         nc.scalar.copy(out=b_bc[:], in_=pb[:])
-        pg = psum.tile([P, 64], F32, tag="acc", bufs=6)
+        pg = psum.tile([P, 64], F32, tag="acc", bufs=4)
         nc.tensor.matmul(pg[:], lhsT=ones[:], rhs=brow[:, 512:576], start=True, stop=True)
         nc.scalar.copy(out=g_bc[:], in_=pg[:])
         w_prep(0)
@@ -251,26 +251,27 @@ def tile_ufoattention_pb_kernel(tc, queries, Wq, bq, gamma, out):
         mx(0)
 
         for s in range(NU + 1):
-            chunks = [i for i in ([0, 1] if s == 0 else [s + 1]) if i < 12]
-            chunks = [(i // 4 + 1, i % 4) for i in chunks]
+            nb = s // 4 + 1
             if s + 1 < NU:
                 mx(s + 1)
-            for bc in chunks:
-                tr(bc[0], bc[1])
+            if s % 4 == 0 and nb < B:
+                for c in range(4):
+                    tr(nb, c)
             if s < NU:
                 e1(s)
                 bn(s)
             if s > 0:
                 e4(s - 1)
                 store(s - 1)
-            for bc in chunks:
-                cp(bc[0], bc[1])
+            if nb < B and s % 4 < 3:
+                cp(nb, s % 4)
+                if s % 4 == 2:
+                    cp(nb, 3)
             if s < NU:
                 sq(s)
                 red(s)
-            for bc in chunks:
-                if bc[1] == 3:
-                    qz_all(bc[0])
+            if nb < B and s % 4 == 2:
+                qz_all(nb)
             if s < 2:
                 w_prep(s + 2)
             if s < NU:

@@ -17,7 +17,6 @@ P = 128
 J = N // P
 FLOPS = 2 * B * N * D * H * DK
 
-PIN = False
 NV = 10
 MG = 10
 MV_LAST = 10
@@ -29,11 +28,9 @@ def tile_ufoattention_pb_kernel(tc, queries, Wq, bq, gamma, out):
     with ExitStack() as ctx:
         const = ctx.enter_context(tc.tile_pool(name="const", bufs=1))
         xq = ctx.enter_context(tc.tile_pool(name="xq", bufs=2))
-        outp = ctx.enter_context(tc.tile_pool(name="outp", bufs=5))
-        small = ctx.enter_context(tc.tile_pool(name="small", bufs=4))
+        outp = ctx.enter_context(tc.tile_pool(name="outp", bufs=7))
+        small = ctx.enter_context(tc.tile_pool(name="small", bufs=6))
         psum = ctx.enter_context(tc.psum_pool(name="psum", bufs=2))
-        if PIN:
-            ctx.enter_context(tc.manual_schedule())
 
         bstage = const.tile([1, 520], BF16)
         nc.sync.dma_start(out=bstage[0:1, 0:512], in_=bq.rearrange("(o n) -> o n", o=1))
@@ -183,12 +180,15 @@ def tile_ufoattention_pb_kernel(tc, queries, Wq, bq, gamma, out):
                     accum_out=ss[:, 16 + i - NV : 17 + i - NV],
                 )
 
-        def red(s):
-            ss, stats = st[s][2], st[s][3]
-            sv = stats[:].rearrange("p n (a c) -> p n a c", c=3)
+        def msq(s):
+            sv = st[s][3][:].rearrange("p n (a c) -> p n a c", c=3)
             nc.scalar.activation(
                 out=sv[:, :, :, 1:2], in_=sv[:, :, :, 1:2], func=ACT.Square, scale=8.0
             )
+
+        def vred(s):
+            ss, stats = st[s][2], st[s][3]
+            sv = stats[:].rearrange("p n (a c) -> p n a c", c=3)
             nc.vector.tensor_reduce(
                 out=ss[:, 16 - NV : 16].rearrange("p (n a) -> p n a", a=2),
                 in_=sv[:, :, :, 1:3], axis=AX.X, op=ALU.add,
@@ -208,7 +208,7 @@ def tile_ufoattention_pb_kernel(tc, queries, Wq, bq, gamma, out):
 
         def e4(s):
             og, rn = st[s][1], st[s][5]
-            last = s == NU - 1
+            last = s >= NU - 2
             wide = MV_LAST if last else MG
             if wide > 0:
                 eng = nc.vector if last else nc.gpsimd
@@ -250,29 +250,31 @@ def tile_ufoattention_pb_kernel(tc, queries, Wq, bq, gamma, out):
         qz(0, 3)
         mx(0)
 
-        for s in range(NU + 1):
+        for s in range(NU + 2):
             nb = s // 4 + 1
             if s + 1 < NU:
                 mx(s + 1)
             if s % 4 == 0 and nb < B:
                 for c in range(4):
                     tr(nb, c)
+            if 1 <= s <= NU:
+                msq(s - 1)
             if s < NU:
                 e1(s)
                 bn(s)
-            if s > 0:
-                e4(s - 1)
-                store(s - 1)
+            if 1 <= s <= NU:
+                vred(s - 1)
             if nb < B and s % 4 < 3:
                 cp(nb, s % 4)
                 if s % 4 == 2:
                     cp(nb, 3)
-            if s < NU:
-                sq(s)
-                red(s)
+            if 1 <= s <= NU:
+                sq(s - 1)
+            if s >= 2:
+                ars(s - 2)
+                e4(s - 2)
+                store(s - 2)
             if nb < B and s % 4 == 2:
                 qz_all(nb)
             if s < 2:
                 w_prep(s + 2)
-            if s < NU:
-                ars(s)

@@ -17,8 +17,8 @@ P = 128
 J = N // P
 FLOPS = 2 * B * N * D * H * DK
 
-NV = 10
-MG = 10
+NVS = (8, 10)
+MG = 11
 MV_LAST = 10
 NU = 16
 
@@ -158,14 +158,14 @@ def tile_ufoattention_pb_kernel(tc, queries, Wq, bq, gamma, out):
                     op=ALU.add,
                 )
             ss = small.tile([P, 32], F32, tag="ss")
-            stats = small.tile([P, NV // 2, 6], F32, tag="stats")
+            stats = small.tile([P, max(NVS) // 2, 6], F32, tag="stats")
             rs = small.tile([P, 16], F32, tag="rs")
             rn = small.tile([P, 16], F32, tag="rn")
             st[s] = (o, o[:].rearrange("p h j d -> p (h j) d"), ss, stats, rs, rn)
 
         def bn(s):
             og, stats = st[s][1], st[s][3]
-            for m in range(NV // 2):
+            for m in range(NVS[s % 2] // 2):
                 nc.vector.bn_stats(
                     out=stats[:, m, :],
                     in_=og[:, 2 * m : 2 * m + 2, :].rearrange("p g d -> p d g"),
@@ -173,6 +173,7 @@ def tile_ufoattention_pb_kernel(tc, queries, Wq, bq, gamma, out):
 
         def sq(s):
             og, ss = st[s][1], st[s][2]
+            NV = NVS[s % 2]
             for i in range(NV, 16):
                 junk = small.tile([P, DK], F32, tag="junk")
                 nc.scalar.activation(
@@ -181,14 +182,15 @@ def tile_ufoattention_pb_kernel(tc, queries, Wq, bq, gamma, out):
                 )
 
         def msq(s):
-            sv = st[s][3][:].rearrange("p n (a c) -> p n a c", c=3)
+            sv = st[s][3][:, 0 : NVS[s % 2] // 2, :].rearrange("p n (a c) -> p n a c", c=3)
             nc.scalar.activation(
                 out=sv[:, :, :, 1:2], in_=sv[:, :, :, 1:2], func=ACT.Square, scale=8.0
             )
 
         def vred(s):
             ss, stats = st[s][2], st[s][3]
-            sv = stats[:].rearrange("p n (a c) -> p n a c", c=3)
+            NV = NVS[s % 2]
+            sv = stats[:, 0 : NV // 2, :].rearrange("p n (a c) -> p n a c", c=3)
             nc.vector.tensor_reduce(
                 out=ss[:, 16 - NV : 16].rearrange("p (n a) -> p n a", a=2),
                 in_=sv[:, :, :, 1:3], axis=AX.X, op=ALU.add,
@@ -197,6 +199,7 @@ def tile_ufoattention_pb_kernel(tc, queries, Wq, bq, gamma, out):
         def ars(s):
             g = s % 4
             ss, rs, rn = st[s][2], st[s][4], st[s][5]
+            NV = NVS[s % 2]
             nc.scalar.activation(
                 out=rs[:], in_=ss[:, 16 - NV : 32 - NV], func=ACT.Abs_reciprocal_sqrt
             )

@@ -17,8 +17,8 @@ P = 128
 J = N // P
 FLOPS = 2 * B * N * D * H * DK
 
-NVS = (8, 10)
-MG = 11
+NVS = (8, 8)
+MG = 12
 MV_LAST = 10
 NU = 16
 

@@ -28,8 +28,8 @@ def tile_ufoattention_pb_kernel(tc, queries, Wq, bq, gamma, out):
     with ExitStack() as ctx:
         const = ctx.enter_context(tc.tile_pool(name="const", bufs=1))
         xq = ctx.enter_context(tc.tile_pool(name="xq", bufs=2))
-        outp = ctx.enter_context(tc.tile_pool(name="outp", bufs=7))
-        small = ctx.enter_context(tc.tile_pool(name="small", bufs=6))
+        outp = ctx.enter_context(tc.tile_pool(name="outp", bufs=9))
+        small = ctx.enter_context(tc.tile_pool(name="small", bufs=8))
         psum = ctx.enter_context(tc.psum_pool(name="psum", bufs=2))
 
         bstage = const.tile([1, 520], BF16)
@@ -253,7 +253,7 @@ def tile_ufoattention_pb_kernel(tc, queries, Wq, bq, gamma, out):
         qz(0, 3)
         mx(0)
 
-        for s in range(NU + 2):
+        for s in range(NU + 3):
             nb = s // 4 + 1
             if s + 1 < NU:
                 mx(s + 1)
@@ -273,10 +273,11 @@ def tile_ufoattention_pb_kernel(tc, queries, Wq, bq, gamma, out):
                     cp(nb, 3)
             if 1 <= s <= NU:
                 sq(s - 1)
-            if s >= 2:
+            if 2 <= s <= NU + 1:
                 ars(s - 2)
-                e4(s - 2)
-                store(s - 2)
+            if s >= 3:
+                e4(s - 3)
+                store(s - 3)
             if nb < B and s % 4 == 2:
                 qz_all(nb)
             if s < 2:

@@ -28,8 +28,8 @@ def tile_ufoattention_pb_kernel(tc, queries, Wq, bq, gamma, out):
     with ExitStack() as ctx:
         const = ctx.enter_context(tc.tile_pool(name="const", bufs=1))
         xq = ctx.enter_context(tc.tile_pool(name="xq", bufs=2))
-        outp = ctx.enter_context(tc.tile_pool(name="outp", bufs=9))
-        small = ctx.enter_context(tc.tile_pool(name="small", bufs=8))
+        outp = ctx.enter_context(tc.tile_pool(name="outp", bufs=11))
+        small = ctx.enter_context(tc.tile_pool(name="small", bufs=10))
         psum = ctx.enter_context(tc.psum_pool(name="psum", bufs=2))
 
         bstage = const.tile([1, 520], BF16)
@@ -253,7 +253,7 @@ def tile_ufoattention_pb_kernel(tc, queries, Wq, bq, gamma, out):
         qz(0, 3)
         mx(0)
 
-        for s in range(NU + 3):
+        for s in range(NU + 4):
             nb = s // 4 + 1
             if s + 1 < NU:
                 mx(s + 1)
@@ -275,9 +275,9 @@ def tile_ufoattention_pb_kernel(tc, queries, Wq, bq, gamma, out):
                 sq(s - 1)
             if 2 <= s <= NU + 1:
                 ars(s - 2)
-            if s >= 3:
-                e4(s - 3)
-                store(s - 3)
+            if s >= 4:
+                e4(s - 4)
+                store(s - 4)
             if nb < B and s % 4 == 2:
                 qz_all(nb)
             if s < 2:

from contextlib import ExitStack

import concourse.mybir as mybir
from concourse.masks import make_identity

F32 = mybir.dt.float32
BF16 = mybir.dt.bfloat16
U32 = mybir.dt.uint32
U8 = mybir.dt.uint8
FP8X4 = mybir.dt.float8_e4m3fn_x4
ACT = mybir.ActivationFunctionType
ALU = mybir.AluOpType
AX = mybir.AxisListType

B, N, D, H, DK = 4, 1024, 512, 8, 64
P = 128
J = N // P
FLOPS = 2 * B * N * D * H * DK

NVS = (8, 8)
MG = 12
MV_LAST = 10
NU = 16


def tile_ufoattention_pb_kernel(tc, queries, Wq, bq, gamma, out):
    nc = tc.nc
    with ExitStack() as ctx:
        const = ctx.enter_context(tc.tile_pool(name="const", bufs=1))
        xq = ctx.enter_context(tc.tile_pool(name="xq", bufs=2))
        outp = ctx.enter_context(tc.tile_pool(name="outp", bufs=11))
        small = ctx.enter_context(tc.tile_pool(name="small", bufs=10))
        psum = ctx.enter_context(tc.psum_pool(name="psum", bufs=2))

        bstage = const.tile([1, 520], BF16)
        nc.sync.dma_start(out=bstage[0:1, 0:512], in_=bq.rearrange("(o n) -> o n", o=1))
        nc.sync.dma_start(out=bstage[0:1, 512:520], in_=gamma.rearrange("a h b c -> a (h b c)"))
        x_sb = [const.tile([P, J * D], BF16, name="x%d" % b) for b in range(B)]
        qv = [queries[b].rearrange("(p j) k -> p (j k)", j=J) for b in range(B)]
        w_raw = const.tile([P, 4, 512], BF16)
        nc.sync.dma_start(out=x_sb[0][:, 0:1024], in_=qv[0][:, 0:1024])
        nc.sync.dma_start(out=x_sb[0][:, 1024:2048], in_=qv[0][:, 1024:2048])
        nc.sync.dma_start(
            out=w_raw[:].rearrange("q (u e) n -> q u (e n)", u=2),
            in_=Wq.rearrange("(u q e) n -> q u (e n)", u=2, e=2),
        )
        nc.sync.dma_start(out=x_sb[0][:, 2048:4096], in_=qv[0][:, 2048:4096])
        nc.sync.dma_start(out=x_sb[1][:, 0:2048], in_=qv[1][:, 0:2048])
        nc.sync.dma_start(out=x_sb[1][:, 2048:4096], in_=qv[1][:, 2048:4096])
        nc.sync.dma_start(out=x_sb[2][:], in_=qv[2])
        nc.sync.dma_start(out=x_sb[3][:], in_=qv[3])

        ident = const.tile([P, P], F32)
        make_identity(nc, ident[:])
        one1 = const.tile([P, 1], F32)
        nc.vector.memset(one1[:], 1.0)
        warm = const.tile([P, 1], F32)
        nc.scalar.activation(out=warm[:], in_=one1[:], func=ACT.Abs_reciprocal_sqrt)
        brow = const.tile([P, 576], BF16)
        nc.vector.memset(brow[:], 0.0)
        ones = const.tile([P, P], BF16)
        nc.vector.memset(ones[:], 1.0)
        nc.vector.tensor_copy(out=brow[0:1, 0:520], in_=bstage[0:1, :])
        b_bc = const.tile([P, 512], F32)
        g_bc = const.tile([P, 64], F32)
        w_grp = const.tile([P, 512, 4], BF16, align_bytes=64)
        w_codes = const.tile([P, 512], U32, align_bytes=64)
        w_scales = const.tile([P, 512], U8, align_bytes=64)

        def w_prep(g):
            cols = slice(g * 128, (g + 1) * 128)
            nc.vector.tensor_copy(
                out=w_grp[:, cols, :], in_=w_raw[:, :, cols].rearrange("q t n -> q n t")
            )
            nc.vector.quantize_mx(
                out=w_codes[:, cols].bitcast(FP8X4),
                scales=w_scales[:, cols],
                in_=w_grp[:, cols, :].rearrange("q n t -> q (n t)"),
            )

        xt = {}
        tps = {}

        def x_tiles(b):
            if b not in xt:
                xg = xq.tile([P, J * P * 4], BF16, tag="xg", align_bytes=64)
                xc = xq.tile([P, J * P], U32, tag="xc", align_bytes=64)
                xs = xq.tile([P, J * P], U8, tag="xs", align_bytes=64)
                xt[b] = (xg, xc, xs)
            return xt[b]

        def tr(b, c):
            xw = x_sb[b][:].bitcast(F32)
            tp = psum.tile([P, 2, 2, P], F32, tag="tp", bufs=4)
            for jj in range(2):
                for u in range(2):
                    o0 = (2 * c + jj) * 256 + u * 128
                    nc.tensor.transpose(tp[:, jj, u, :], xw[:, o0 : o0 + 128], ident[:])
            tps[(b, c)] = tp

        def cp(b, c):
            xg = x_tiles(b)[0]
            nc.scalar.copy(
                out=xg[:].bitcast(F32)[:, c * 512 : (c + 1) * 512].rearrange(
                    "p (jj n u) -> p jj n u", jj=2, u=2
                ),
                in_=tps[(b, c)][:].rearrange("p jj u n -> p jj n u"),
            )

        def qz(b, c):
            xg, xc, xs = x_tiles(b)
            nc.vector.quantize_mx(
                out=xc[:, c * 256 : (c + 1) * 256].bitcast(FP8X4),
                scales=xs[:, c * 256 : (c + 1) * 256],
                in_=xg[:, c * 1024 : (c + 1) * 1024],
            )

        def qz_all(b):
            xg, xc, xs = x_tiles(b)
            nc.vector.quantize_mx(out=xc[:].bitcast(FP8X4), scales=xs[:], in_=xg[:])

        accs = {}
        st = {}

        def mx(s):
            b, g = divmod(s, 4)
            xc, xs = x_tiles(b)[1:]
            wcols = slice(g * 128, (g + 1) * 128)
            for k in range(2):
                acc = psum.tile([P, 4, P], F32, tag="acc", bufs=4)
                for jj in range(4):
                    tcols = slice((4 * k + jj) * P, (4 * k + jj + 1) * P)
                    nc.tensor.matmul_mx(
                        out=acc[:, jj, :],
                        lhsT=xc[:, tcols].bitcast(FP8X4),
                        lhsT_scale=xs[:, tcols],
                        rhs=w_codes[:, wcols].bitcast(FP8X4),
                        rhs_scale=w_scales[:, wcols],
                        start=True,
                        stop=True,
                    )
                accs[(s, k)] = acc

        def e1(s):
            g = s % 4
            o = outp.tile([P, 2, J, DK], F32, tag="o")
            bias = (
                b_bc[:, g * 128 : (g + 1) * 128]
                .rearrange("p (h d) -> p h d", h=2)
                .unsqueeze(1)
                .to_broadcast([P, 4, 2, DK])
            )
            for k in range(2):
                nc.vector.tensor_tensor(
                    out=o[:, :, 4 * k : 4 * k + 4, :].rearrange("p h j d -> p j h d"),
                    in0=accs[(s, k)][:].rearrange("p j (h d) -> p j h d", h=2),
                    in1=bias,
                    op=ALU.add,
                )
            ss = small.tile([P, 32], F32, tag="ss")
            stats = small.tile([P, max(NVS) // 2, 6], F32, tag="stats")
            rs = small.tile([P, 16], F32, tag="rs")
            rn = small.tile([P, 16], F32, tag="rn")
            st[s] = (o, o[:].rearrange("p h j d -> p (h j) d"), ss, stats, rs, rn)

        def bn(s):
            og, stats = st[s][1], st[s][3]
            for m in range(NVS[s % 2] // 2):
                nc.vector.bn_stats(
                    out=stats[:, m, :],
                    in_=og[:, 2 * m : 2 * m + 2, :].rearrange("p g d -> p d g"),
                )

        def sq(s):
            og, ss = st[s][1], st[s][2]
            NV = NVS[s % 2]
            for i in range(NV, 16):
                junk = small.tile([P, DK], F32, tag="junk")
                nc.scalar.activation(
                    out=junk[:], in_=og[:, i, :], func=ACT.Square,
                    accum_out=ss[:, 16 + i - NV : 17 + i - NV],
                )

        def msq(s):
            sv = st[s][3][:, 0 : NVS[s % 2] // 2, :].rearrange("p n (a c) -> p n a c", c=3)
            nc.scalar.activation(
                out=sv[:, :, :, 1:2], in_=sv[:, :, :, 1:2], func=ACT.Square, scale=8.0
            )

        def vred(s):
            ss, stats = st[s][2], st[s][3]
            NV = NVS[s % 2]
            sv = stats[:, 0 : NV // 2, :].rearrange("p n (a c) -> p n a c", c=3)
            nc.vector.tensor_reduce(
                out=ss[:, 16 - NV : 16].rearrange("p (n a) -> p n a", a=2),
                in_=sv[:, :, :, 1:3], axis=AX.X, op=ALU.add,
            )

        def ars(s):
            g = s % 4
            ss, rs, rn = st[s][2], st[s][4], st[s][5]
            NV = NVS[s % 2]
            nc.scalar.activation(
                out=rs[:], in_=ss[:, 16 - NV : 32 - NV], func=ACT.Abs_reciprocal_sqrt
            )
            for hh in range(2):
                nc.scalar.activation(
                    out=rn[:, hh * J : (hh + 1) * J], in_=rs[:, hh * J : (hh + 1) * J],
                    func=ACT.Copy, scale=g_bc[:, 2 * g + hh : 2 * g + hh + 1],
                )

        def e4(s):
            og, rn = st[s][1], st[s][5]
            last = s >= NU - 2
            wide = MV_LAST if last else MG
            if wide > 0:
                eng = nc.vector if last else nc.gpsimd
                eng.tensor_tensor(
                    out=og[:, 0:wide, :], in0=og[:, 0:wide, :],
                    in1=rn[:, 0:wide].unsqueeze(2).to_broadcast([P, wide, DK]), op=ALU.mult,
                )
            for i in range(wide, 16):
                nc.scalar.activation(
                    out=og[:, i, :], in_=og[:, i, :], func=ACT.Copy, scale=rn[:, i : i + 1]
                )

        def store(s):
            b, g = divmod(s, 4)
            nc.sync.dma_start(
                out=out[b, 2 * g : 2 * g + 2].rearrange("h (p j) d -> p h (j d)", j=J),
                in_=st[s][0][:].rearrange("p h j d -> p h (j d)"),
            )

        tr(0, 0)
        cp(0, 0)
        qz(0, 0)
        tr(0, 1)
        cp(0, 1)
        qz(0, 1)
        pb = psum.tile([P, 512], F32, tag="acc", bufs=4)
        nc.tensor.matmul(pb[:], lhsT=ones[:], rhs=brow[:, 0:512], start=True, stop=True)
        nc.scalar.copy(out=b_bc[:], in_=pb[:])
        pg = psum.tile([P, 64], F32, tag="acc", bufs=4)
        nc.tensor.matmul(pg[:], lhsT=ones[:], rhs=brow[:, 512:576], start=True, stop=True)
        nc.scalar.copy(out=g_bc[:], in_=pg[:])
        w_prep(0)
        tr(0, 2)
        cp(0, 2)
        tr(0, 3)
        cp(0, 3)
        w_prep(1)
        qz(0, 2)
        qz(0, 3)
        mx(0)

        for s in range(NU + 4):
            nb = s // 4 + 1
            if s + 1 < NU:
                mx(s + 1)
            if s % 4 == 0 and nb < B:
                for c in range(4):
                    tr(nb, c)
            if 1 <= s <= NU:
                msq(s - 1)
            if s < NU:
                e1(s)
                bn(s)
            if 1 <= s <= NU:
                vred(s - 1)
            if nb < B and s % 4 < 3:
                cp(nb, s % 4)
                if s % 4 == 2:
                    cp(nb, 3)
            if 1 <= s <= NU:
                sq(s - 1)
            if 2 <= s <= NU + 1:
                ars(s - 2)
            if s >= 4:
                e4(s - 4)
                store(s - 4)
            if nb < B and s % 4 == 2:
                qz_all(nb)
            if s < 2:
                w_prep(s + 2)
